import numpy as np
import ml_dtypes


def mxq(x, axis, fmt="e4m3"):
    dtype, down = {"e4m3": (ml_dtypes.float8_e4m3fn, 7), "e5m2": (ml_dtypes.float8_e5m2, 14)}[fmt]
    v = np.moveaxis(np.asarray(x, np.float32).astype(ml_dtypes.bfloat16).astype(np.float64), axis, -1)
    blocks = v.reshape(v.shape[:-1] + (-1, 32))
    amax = np.abs(blocks).max(-1, keepdims=True)
    byte = np.maximum(np.where(amax > 0, np.frexp(amax)[1] - 1 + 127, 0) - down, 1)
    scale = np.exp2(byte - 127.0)
    codes = (blocks / scale).astype(np.float32).astype(dtype).astype(np.float64)
    return np.moveaxis((codes * scale).reshape(v.shape), -1, axis)


WIDE = False


def mx_kscale(k):
    if not WIDE:
        return np.ones(k)
    levels = np.array([10, -10, 5, -5, 0])
    a = np.random.permutation(np.resize(levels, k // 512 * 4)).reshape(k // 512, 4)
    idx = np.arange(k)
    return np.exp2(a[idx // 512, idx % 128 // 32])


BF16 = ml_dtypes.bfloat16


def bf(x):
    return np.asarray(x, np.float32).astype(BF16)


def f64(x):
    return np.asarray(x).astype(np.float64)


B, T, E, H, DK, C = 4, 1024, 512, 4, 128, 512
DV = 2 * DK
F = H * DV
EPS = 1e-5


def setup_inputs():
    s, t = mx_kscale(E), mx_kscale(F)
    o = np.random.standard_normal((B, T, H, DV)) * 5.0 * np.exp(0.5 * np.random.standard_normal((B, T, H, 1)))
    return {"o_ret": bf(o),
            "x": bf(np.random.standard_normal((B, T, E)) * s),
            "Wg": bf(np.random.standard_normal((E, F)) / np.sqrt(E) / s[:, None] * t),
            "gn_weight": bf(1.0 + 0.1 * np.random.standard_normal(DV)),
            "Wo": bf(np.random.standard_normal((F, E)) / np.sqrt(F) / t[:, None])}


def reference(o_ret, x, Wg, gn_weight, Wo):
    o = f64(o_ret)
    rms = np.sqrt(np.mean(o * o, axis=-1, keepdims=True) + EPS)
    o = o / rms * f64(gn_weight)
    g = mxq(f64(x), 2, "e4m3") @ mxq(f64(Wg), 0, "e4m3")
    h = o.reshape(B, T, F) * g
    return mxq(h, 2, "e4m3") @ mxq(f64(Wo), 0, "e4m3")

@@ -1,0 +1,280 @@
+from contextlib import ExitStack
+
+import concourse.mybir as mybir
+from concourse.masks import make_identity
+
+F32 = mybir.dt.float32
+BF16 = mybir.dt.bfloat16
+U32 = mybir.dt.uint32
+U8 = mybir.dt.uint8
+FP8X4 = mybir.dt.float8_e4m3fn_x4
+
+P = 128
+PACK = 4
+K_PASS = P * PACK
+BANK = 512
+
+TOKENS = 4 * 1024
+E = 512
+HEADS = 4
+DV = 256
+F = HEADS * DV
+EPS = 1e-5
+
+TILES = TOKENS // P
+GROUP = 4
+GROUPS = TILES // GROUP
+F_BANKS = F // BANK
+F_PASSES = F // K_PASS
+HEADS_PER_BANK = BANK // DV
+
+FLOPS = 2 * TOKENS * E * F + 2 * TOKENS * F * E
+
+SQUARES_LEAD = 6
+INVERT_RMS_LEAD = 5
+X_TRANSPOSE_LEAD = 4
+X_COPY_LEAD = 3
+X_QUANTISE_LEAD = 2
+GATE_MATMUL_LEAD = 1
+GATE_MULTIPLY_LEAD = 0
+H_TRANSPOSE_LEAD = -1
+H_SCALE_LEAD = -1
+H_QUANTISE_LEAD = -2
+OUT_MATMUL_LEAD = -2
+OUT_COPY_LEAD = -3
+FIRST_STEP = -SQUARES_LEAD
+LAST_STEP = TILES - 1 - OUT_COPY_LEAD
+
+
+def tile_multiscaleretention_pc_t_kernel(tc, o_ret, x, Wg, gn_weight, Wo, out):
+    nc = tc.nc
+    mult = mybir.AluOpType.mult
+    func = mybir.ActivationFunctionType
+
+    x_dram = x.flatten_outer_dims().rearrange("(n p i) e -> n p (i e)", p=P, i=GROUP)
+    o_dram = o_ret.rearrange("b t h d -> (b t) (h d)").rearrange(
+        "(n p i) f -> n p (i f)", p=P, i=GROUP
+    )
+    out_dram = out.flatten_outer_dims().rearrange("(n p i) e -> n p (i e)", p=P, i=GROUP)
+
+    with ExitStack() as ctx:
+        keep = ctx.enter_context(tc.tile_pool(name="keep", bufs=1))
+        stream = ctx.enter_context(tc.tile_pool(name="stream", bufs=3))
+        psum = ctx.enter_context(tc.psum_pool(name="psum", bufs=2))
+
+        x_sb = [keep.tile([P, GROUP * E], BF16, name="x_sb%d" % grp) for grp in range(GROUPS)]
+        o_sb = [keep.tile([P, GROUP * F], BF16, name="o_sb%d" % grp) for grp in range(GROUPS)]
+        wg_raw = keep.tile([P, PACK, F], BF16)
+        wo_raw = keep.tile([P, F_PASSES, PACK, E], BF16)
+        gn_cols = keep.tile([P, DV // P], BF16)
+
+        nc.sync.dma_start(out=o_sb[0][:], in_=o_dram[0])
+        nc.sync.dma_start(
+            out=wg_raw[:].rearrange("p (u e) f -> p u e f", e=2),
+            in_=Wg.rearrange("(u p e) f -> p u e f", p=P, e=2),
+        )
+        nc.sync.dma_start(out=x_sb[0][:], in_=x_dram[0])
+        with nc.allow_non_contiguous_dma(reason="256 elements, one to a partition and column"):
+            nc.sync.dma_start(out=gn_cols[:], in_=gn_weight.rearrange("(s p) -> p s", p=P))
+        nc.sync.dma_start(out=wo_raw[:], in_=Wo.rearrange("(c t p) e -> p c t e", p=P, t=PACK))
+        for grp in range(1, GROUPS):
+            nc.sync.dma_start(out=x_sb[grp][:], in_=x_dram[grp])
+            nc.sync.dma_start(out=o_sb[grp][:], in_=o_dram[grp])
+
+        identity = keep.tile([P, P], F32)
+        make_identity(nc, identity[:])
+        eps = keep.tile([P, 1], F32)
+        nc.vector.memset(eps[:], EPS)
+        gn_word = keep.tile([P, PACK], F32)
+        nc.vector.tensor_copy(
+            out=gn_word[:].rearrange("p (a s) -> p a s", s=DV // P),
+            in_=gn_cols[:].unsqueeze(1).to_broadcast([P, PACK * P // DV, DV // P]),
+        )
+
+        wg_grouped = keep.tile([P, F, PACK], BF16, align_bytes=64)
+        wg_codes = keep.tile([P, F], U32, align_bytes=64)
+        wg_scales = keep.tile([P, F], U8, align_bytes=64)
+        wo_grouped = keep.tile([P, F_PASSES, E, PACK], BF16, align_bytes=64)
+        wo_codes = keep.tile([P, F_PASSES, E], U32, align_bytes=64)
+        wo_scales = keep.tile([P, F_PASSES, E], U8, align_bytes=64)
+
+        def quantise_wg():
+            for n in range(F_BANKS):
+                cols = slice(n * BANK, (n + 1) * BANK)
+                nc.vector.tensor_copy(
+                    out=wg_grouped[:, cols, :], in_=wg_raw[:, :, cols].rearrange("p t f -> p f t")
+                )
+            for n in range(F_BANKS):
+                cols = slice(n * BANK, (n + 1) * BANK)
+                nc.vector.quantize_mx(
+                    out=wg_codes[:, cols].bitcast(FP8X4),
+                    scales=wg_scales[:, cols],
+                    in_=wg_grouped[:, cols, :].rearrange("p f t -> p (f t)"),
+                )
+
+        def quantise_wo():
+            for c in range(F_PASSES):
+                nc.vector.tensor_copy(
+                    out=wo_grouped[:, c, :, :], in_=wo_raw[:, c, :, :].rearrange("p t e -> p e t")
+                )
+            for c in range(F_PASSES):
+                nc.vector.quantize_mx(
+                    out=wo_codes[:, c, :].bitcast(FP8X4),
+                    scales=wo_scales[:, c, :],
+                    in_=wo_grouped[:, c, :, :].rearrange("p e t -> p (e t)"),
+                )
+
+        sums, rms, inv_rms = {}, {}, {}
+        x_t, x_grouped, x_codes, x_scales = {}, {}, {}, {}
+        g_ps, h_f32, h_t, h_grouped, h_codes, h_scales = {}, {}, {}, {}, {}, {}
+        out_ps = {}
+
+        def sum_squares(j):
+            grp, i = divmod(j, GROUP)
+            if i == 0:
+                sums[grp] = stream.tile([P, GROUP * HEADS], F32, name="sums")
+            for head in range(HEADS):
+                squares = stream.tile([P, DV], BF16, name="squares")
+                nc.scalar.activation(
+                    out=squares[:],
+                    in_=o_sb[grp][:, i * F + head * DV : i * F + (head + 1) * DV],
+                    func=func.Square,
+                    accum_out=sums[grp][:, i * HEADS + head : i * HEADS + head + 1],
+                )
+            if i == GROUP - 1:
+                rms[grp] = stream.tile([P, GROUP * HEADS], F32, name="rms")
+                nc.scalar.activation(
+                    out=rms[grp][:], in_=sums[grp][:], func=func.Sqrt, scale=1.0 / DV, bias=eps[:]
+                )
+
+        def invert_rms(j):
+            grp, i = divmod(j, GROUP)
+            if i == GROUP - 1:
+                inv_rms[grp] = stream.tile([P, GROUP * HEADS], F32, name="inv_rms")
+                nc.vector.reciprocal(out=inv_rms[grp][:], in_=rms[grp][:])
+
+        def transpose_x(j):
+            grp, i = divmod(j, GROUP)
+            words = x_sb[grp][:].bitcast(F32)
+            x_t[j] = psum.tile([P, 2, P], F32, name="x_t")
+            for u in range(2):
+                first = i * (E // 2) + u * P
+                nc.tensor.transpose(x_t[j][:, u, :], words[:, first : first + P], identity[:])
+
+        def copy_x(j):
+            x_grouped[j] = stream.tile([P, P * PACK], BF16, name="x_grouped", align_bytes=64)
+            nc.scalar.copy(
+                out=x_grouped[j][:].bitcast(F32).rearrange("p (r u) -> p r u", u=2),
+                in_=x_t[j][:].rearrange("p u r -> p r u"),
+            )
+
+        def quantise_x(j):
+            x_codes[j] = stream.tile([P, P], U32, name="x_codes", align_bytes=64)
+            x_scales[j] = stream.tile([P, P], U8, name="x_scales", align_bytes=64)
+            nc.vector.quantize_mx(
+                out=x_codes[j][:].bitcast(FP8X4), scales=x_scales[j][:], in_=x_grouped[j][:]
+            )
+
+        def gate_matmul(j):
+            g_ps[j] = []
+            for n in range(F_BANKS):
+                cols = slice(n * BANK, (n + 1) * BANK)
+                bank = psum.tile([P, BANK], F32, name="g_ps")
+                nc.tensor.matmul_mx(
+                    out=bank[:],
+                    lhsT=x_codes[j][:].bitcast(FP8X4),
+                    lhsT_scale=x_scales[j][:],
+                    rhs=wg_codes[:, cols].bitcast(FP8X4),
+                    rhs_scale=wg_scales[:, cols],
+                    start=True,
+                    stop=True,
+                )
+                g_ps[j].append(bank)
+
+        def gate_multiply(j):
+            grp, i = divmod(j, GROUP)
+            h_f32[j] = stream.tile([P, F], F32, name="h_f32")
+            for head in range(HEADS):
+                n, a = divmod(head, HEADS_PER_BANK)
+                nc.vector.scalar_tensor_tensor(
+                    out=h_f32[j][:, head * DV : (head + 1) * DV],
+                    in0=g_ps[j][n][:, a * DV : (a + 1) * DV],
+                    scalar=inv_rms[grp][:, i * HEADS + head : i * HEADS + head + 1],
+                    in1=o_sb[grp][:, i * F + head * DV : i * F + (head + 1) * DV],
+                    op0=mult,
+                    op1=mult,
+                )
+
+        def transpose_h(j):
+            h_t[j] = []
+            for c in range(F_PASSES):
+                bank = psum.tile([P, PACK, P], F32, name="h_t")
+                for t in range(PACK):
+                    first = c * K_PASS + t * P
+                    nc.tensor.transpose(bank[:, t, :], h_f32[j][:, first : first + P], identity[:])
+                h_t[j].append(bank)
+
+        def scale_h(j):
+            h_grouped[j] = stream.tile([P, F_PASSES, P, PACK], BF16, name="h_grouped", align_bytes=64)
+            for c in range(F_PASSES):
+                nc.vector.tensor_tensor(
+                    out=h_grouped[j][:, c, :, :],
+                    in0=h_t[j][c][:].rearrange("p t r -> p r t"),
+                    in1=gn_word[:].unsqueeze(1).to_broadcast([P, P, PACK]),
+                    op=mult,
+                )
+
+        def quantise_h(j):
+            h_codes[j] = stream.tile([P, F_PASSES * P], U32, name="h_codes", align_bytes=64)
+            h_scales[j] = stream.tile([P, F_PASSES * P], U8, name="h_scales", align_bytes=64)
+            nc.vector.quantize_mx(
+                out=h_codes[j][:].bitcast(FP8X4),
+                scales=h_scales[j][:],
+                in_=h_grouped[j][:].rearrange("p c r t -> p (c r t)"),
+            )
+
+        def out_matmul(j):
+            out_ps[j] = psum.tile([P, E], F32, name="out_ps")
+            for c in range(F_PASSES):
+                tokens = slice(c * P, (c + 1) * P)
+                nc.tensor.matmul_mx(
+                    out=out_ps[j][:],
+                    lhsT=h_codes[j][:, tokens].bitcast(FP8X4),
+                    lhsT_scale=h_scales[j][:, tokens],
+                    rhs=wo_codes[:, c, :].bitcast(FP8X4),
+                    rhs_scale=wo_scales[:, c, :],
+                    start=(c == 0),
+                    stop=(c == F_PASSES - 1),
+                )
+
+        def copy_out(j):
+            grp, i = divmod(j, GROUP)
+            out_sb = stream.tile([P, E], F32, name="out_sb")
+            nc.scalar.copy(out=out_sb[:], in_=out_ps[j][:])
+            nc.sync.dma_start(out=out_dram[grp][:, i * E : (i + 1) * E], in_=out_sb[:])
+
+        def run(stage, j):
+            if 0 <= j < TILES:
+                stage(j)
+
+        def pipeline_step(step):
+            run(transpose_x, step + X_TRANSPOSE_LEAD)
+            run(transpose_h, step + H_TRANSPOSE_LEAD)
+            run(copy_x, step + X_COPY_LEAD)
+            run(copy_out, step + OUT_COPY_LEAD)
+            run(sum_squares, step + SQUARES_LEAD)
+            run(gate_multiply, step + GATE_MULTIPLY_LEAD)
+            run(gate_matmul, step + GATE_MATMUL_LEAD)
+            run(invert_rms, step + INVERT_RMS_LEAD)
+            run(quantise_x, step + X_QUANTISE_LEAD)
+            run(quantise_h, step + H_QUANTISE_LEAD)
+            run(out_matmul, step + OUT_MATMUL_LEAD)
+            run(scale_h, step + H_SCALE_LEAD)
+
+        with tc.manual_schedule():
+            quantise_wg()
+            for step in range(FIRST_STEP, 1):
+                pipeline_step(step)
+            quantise_wo()
+            for step in range(1, LAST_STEP + 1):
+                pipeline_step(step)

@@ -27,6 +27,9 @@ GROUPS = TILES // GROUP
 F_BANKS = F // BANK
 F_PASSES = F // K_PASS
 HEADS_PER_BANK = BANK // DV
+HALVES = DV // P
+HEADS_PER_PASS = K_PASS // DV
+SCALAR_EVERY = 5
 
 FLOPS = 2 * TOKENS * E * F + 2 * TOKENS * F * E
 
@@ -66,7 +69,7 @@ def tile_multiscaleretention_pc_t_kernel(tc, o_ret, x, Wg, gn_weight, Wo, out):
         o_sb = [keep.tile([P, GROUP * F], BF16, name="o_sb%d" % grp) for grp in range(GROUPS)]
         wg_raw = keep.tile([P, PACK, F], BF16)
         wo_raw = keep.tile([P, F_PASSES, PACK, E], BF16)
-        gn_cols = keep.tile([P, DV // P], BF16)
+        gn_cols = keep.tile([P, HALVES], BF16)
 
         nc.sync.dma_start(out=o_sb[0][:], in_=o_dram[0])
         nc.sync.dma_start(
@@ -76,7 +79,7 @@ def tile_multiscaleretention_pc_t_kernel(tc, o_ret, x, Wg, gn_weight, Wo, out):
         nc.sync.dma_start(out=x_sb[0][:], in_=x_dram[0])
         with nc.allow_non_contiguous_dma(reason="256 elements, one to a partition and column"):
             nc.sync.dma_start(out=gn_cols[:], in_=gn_weight.rearrange("(s p) -> p s", p=P))
-        nc.sync.dma_start(out=wo_raw[:], in_=Wo.rearrange("(c t p) e -> p c t e", p=P, t=PACK))
+        nc.sync.dma_start(out=wo_raw[:], in_=Wo.rearrange("(c b p) e -> p c b e", p=P, b=PACK))
         for grp in range(1, GROUPS):
             nc.sync.dma_start(out=x_sb[grp][:], in_=x_dram[grp])
             nc.sync.dma_start(out=o_sb[grp][:], in_=o_dram[grp])
@@ -87,8 +90,8 @@ def tile_multiscaleretention_pc_t_kernel(tc, o_ret, x, Wg, gn_weight, Wo, out):
         nc.vector.memset(eps[:], EPS)
         gn_word = keep.tile([P, PACK], F32)
         nc.vector.tensor_copy(
-            out=gn_word[:].rearrange("p (a s) -> p a s", s=DV // P),
-            in_=gn_cols[:].unsqueeze(1).to_broadcast([P, PACK * P // DV, DV // P]),
+            out=gn_word[:].rearrange("p (s a) -> p s a", s=HALVES),
+            in_=gn_cols[:].unsqueeze(2).to_broadcast([P, HALVES, HEADS_PER_PASS]),
         )
 
         wg_grouped = keep.tile([P, F, PACK], BF16, align_bytes=64)
@@ -115,7 +118,8 @@ def tile_multiscaleretention_pc_t_kernel(tc, o_ret, x, Wg, gn_weight, Wo, out):
         def quantise_wo():
             for c in range(F_PASSES):
                 nc.vector.tensor_copy(
-                    out=wo_grouped[:, c, :, :], in_=wo_raw[:, c, :, :].rearrange("p t e -> p e t")
+                    out=wo_grouped[:, c, :, :].rearrange("p e (s a) -> p e s a", s=HALVES),
+                    in_=wo_raw[:, c, :, :].rearrange("p (a s) e -> p e s a", s=HALVES),
                 )
             for c in range(F_PASSES):
                 nc.vector.quantize_mx(
@@ -209,20 +213,35 @@ def tile_multiscaleretention_pc_t_kernel(tc, o_ret, x, Wg, gn_weight, Wo, out):
             h_t[j] = []
             for c in range(F_PASSES):
                 bank = psum.tile([P, PACK, P], F32, name="h_t")
-                for t in range(PACK):
-                    first = c * K_PASS + t * P
-                    nc.tensor.transpose(bank[:, t, :], h_f32[j][:, first : first + P], identity[:])
+                for s in range(HALVES):
+                    for a in range(HEADS_PER_PASS):
+                        first = c * K_PASS + a * DV + s * P
+                        nc.tensor.transpose(
+                            bank[:, s * HEADS_PER_PASS + a, :],
+                            h_f32[j][:, first : first + P],
+                            identity[:],
+                        )
                 h_t[j].append(bank)
 
         def scale_h(j):
             h_grouped[j] = stream.tile([P, F_PASSES, P, PACK], BF16, name="h_grouped", align_bytes=64)
             for c in range(F_PASSES):
-                nc.vector.tensor_tensor(
-                    out=h_grouped[j][:, c, :, :],
-                    in0=h_t[j][c][:].rearrange("p t r -> p r t"),
-                    in1=gn_word[:].unsqueeze(1).to_broadcast([P, P, PACK]),
-                    op=mult,
-                )
+                if (j * F_PASSES + c) % SCALAR_EVERY == SCALAR_EVERY - 1:
+                    for s in range(HALVES):
+                        values = slice(s * HEADS_PER_PASS, (s + 1) * HEADS_PER_PASS)
+                        nc.scalar.activation(
+                            out=h_grouped[j][:, c, :, values],
+                            in_=h_t[j][c][:, values, :].rearrange("p a r -> p r a"),
+                            func=func.Copy,
+                            scale=gn_word[:, s * HEADS_PER_PASS : s * HEADS_PER_PASS + 1],
+                        )
+                else:
+                    nc.vector.tensor_tensor(
+                        out=h_grouped[j][:, c, :, :],
+                        in0=h_t[j][c][:].rearrange("p t r -> p r t"),
+                        in1=gn_word[:].unsqueeze(1).to_broadcast([P, P, PACK]),
+                        op=mult,
+                    )
 
         def quantise_h(j):
             h_codes[j] = stream.tile([P, F_PASSES * P], U32, name="h_codes", align_bytes=64)

@@ -29,7 +29,7 @@ F_PASSES = F // K_PASS
 HEADS_PER_BANK = BANK // DV
 HALVES = DV // P
 HEADS_PER_PASS = K_PASS // DV
-SCALAR_EVERY = 5
+SCALAR_EVERY = 6
 
 FLOPS = 2 * TOKENS * E * F + 2 * TOKENS * F * E
 
@@ -72,10 +72,13 @@ def tile_multiscaleretention_pc_t_kernel(tc, o_ret, x, Wg, gn_weight, Wo, out):
         gn_cols = keep.tile([P, HALVES], BF16)
 
         nc.sync.dma_start(out=o_sb[0][:], in_=o_dram[0])
-        nc.sync.dma_start(
-            out=wg_raw[:].rearrange("p (u e) f -> p u e f", e=2),
-            in_=Wg.rearrange("(u p e) f -> p u e f", p=P, e=2),
-        )
+        for n in range(F_BANKS):
+            cols = slice(n * BANK, (n + 1) * BANK)
+            for u in range(2):
+                nc.sync.dma_start(
+                    out=wg_raw[:, 2 * u : 2 * u + 2, cols],
+                    in_=Wg[2 * P * u : 2 * P * (u + 1), cols].rearrange("(p e) f -> p e f", e=2),
+                )
         nc.sync.dma_start(out=x_sb[0][:], in_=x_dram[0])
         with nc.allow_non_contiguous_dma(reason="256 elements, one to a partition and column"):
             nc.sync.dma_start(out=gn_cols[:], in_=gn_weight.rearrange("(s p) -> p s", p=P))
@@ -88,6 +91,8 @@ def tile_multiscaleretention_pc_t_kernel(tc, o_ret, x, Wg, gn_weight, Wo, out):
         make_identity(nc, identity[:])
         eps = keep.tile([P, 1], F32)
         nc.vector.memset(eps[:], EPS)
+        first_sqrt = keep.tile([P, 1], F32)
+        nc.scalar.activation(out=first_sqrt[:], in_=eps[:], func=func.Sqrt)
         gn_word = keep.tile([P, PACK], F32)
         nc.vector.tensor_copy(
             out=gn_word[:].rearrange("p (s a) -> p s a", s=HALVES),

from contextlib import ExitStack

import concourse.mybir as mybir
from concourse.masks import make_identity

F32 = mybir.dt.float32
BF16 = mybir.dt.bfloat16
U32 = mybir.dt.uint32
U8 = mybir.dt.uint8
FP8X4 = mybir.dt.float8_e4m3fn_x4

P = 128
PACK = 4
K_PASS = P * PACK
BANK = 512

TOKENS = 4 * 1024
E = 512
HEADS = 4
DV = 256
F = HEADS * DV
EPS = 1e-5

TILES = TOKENS // P
GROUP = 4
GROUPS = TILES // GROUP
F_BANKS = F // BANK
F_PASSES = F // K_PASS
HEADS_PER_BANK = BANK // DV
HALVES = DV // P
HEADS_PER_PASS = K_PASS // DV
SCALAR_EVERY = 6

FLOPS = 2 * TOKENS * E * F + 2 * TOKENS * F * E

SQUARES_LEAD = 6
INVERT_RMS_LEAD = 5
X_TRANSPOSE_LEAD = 4
X_COPY_LEAD = 3
X_QUANTISE_LEAD = 2
GATE_MATMUL_LEAD = 1
GATE_MULTIPLY_LEAD = 0
H_TRANSPOSE_LEAD = -1
H_SCALE_LEAD = -1
H_QUANTISE_LEAD = -2
OUT_MATMUL_LEAD = -2
OUT_COPY_LEAD = -3
FIRST_STEP = -SQUARES_LEAD
LAST_STEP = TILES - 1 - OUT_COPY_LEAD


def tile_multiscaleretention_pc_t_kernel(tc, o_ret, x, Wg, gn_weight, Wo, out):
    nc = tc.nc
    mult = mybir.AluOpType.mult
    func = mybir.ActivationFunctionType

    x_dram = x.flatten_outer_dims().rearrange("(n p i) e -> n p (i e)", p=P, i=GROUP)
    o_dram = o_ret.rearrange("b t h d -> (b t) (h d)").rearrange(
        "(n p i) f -> n p (i f)", p=P, i=GROUP
    )
    out_dram = out.flatten_outer_dims().rearrange("(n p i) e -> n p (i e)", p=P, i=GROUP)

    with ExitStack() as ctx:
        keep = ctx.enter_context(tc.tile_pool(name="keep", bufs=1))
        stream = ctx.enter_context(tc.tile_pool(name="stream", bufs=3))
        psum = ctx.enter_context(tc.psum_pool(name="psum", bufs=2))

        x_sb = [keep.tile([P, GROUP * E], BF16, name="x_sb%d" % grp) for grp in range(GROUPS)]
        o_sb = [keep.tile([P, GROUP * F], BF16, name="o_sb%d" % grp) for grp in range(GROUPS)]
        wg_raw = keep.tile([P, PACK, F], BF16)
        wo_raw = keep.tile([P, F_PASSES, PACK, E], BF16)
        gn_cols = keep.tile([P, HALVES], BF16)

        nc.sync.dma_start(out=o_sb[0][:], in_=o_dram[0])
        for n in range(F_BANKS):
            cols = slice(n * BANK, (n + 1) * BANK)
            for u in range(2):
                nc.sync.dma_start(
                    out=wg_raw[:, 2 * u : 2 * u + 2, cols],
                    in_=Wg[2 * P * u : 2 * P * (u + 1), cols].rearrange("(p e) f -> p e f", e=2),
                )
        nc.sync.dma_start(out=x_sb[0][:], in_=x_dram[0])
        with nc.allow_non_contiguous_dma(reason="256 elements, one to a partition and column"):
            nc.sync.dma_start(out=gn_cols[:], in_=gn_weight.rearrange("(s p) -> p s", p=P))
        nc.sync.dma_start(out=wo_raw[:], in_=Wo.rearrange("(c b p) e -> p c b e", p=P, b=PACK))
        for grp in range(1, GROUPS):
            nc.sync.dma_start(out=x_sb[grp][:], in_=x_dram[grp])
            nc.sync.dma_start(out=o_sb[grp][:], in_=o_dram[grp])

        identity = keep.tile([P, P], F32)
        make_identity(nc, identity[:])
        eps = keep.tile([P, 1], F32)
        nc.vector.memset(eps[:], EPS)
        first_sqrt = keep.tile([P, 1], F32)
        nc.scalar.activation(out=first_sqrt[:], in_=eps[:], func=func.Sqrt)
        gn_word = keep.tile([P, PACK], F32)
        nc.vector.tensor_copy(
            out=gn_word[:].rearrange("p (s a) -> p s a", s=HALVES),
            in_=gn_cols[:].unsqueeze(2).to_broadcast([P, HALVES, HEADS_PER_PASS]),
        )

        wg_grouped = keep.tile([P, F, PACK], BF16, align_bytes=64)
        wg_codes = keep.tile([P, F], U32, align_bytes=64)
        wg_scales = keep.tile([P, F], U8, align_bytes=64)
        wo_grouped = keep.tile([P, F_PASSES, E, PACK], BF16, align_bytes=64)
        wo_codes = keep.tile([P, F_PASSES, E], U32, align_bytes=64)
        wo_scales = keep.tile([P, F_PASSES, E], U8, align_bytes=64)

        def quantise_wg():
            for n in range(F_BANKS):
                cols = slice(n * BANK, (n + 1) * BANK)
                nc.vector.tensor_copy(
                    out=wg_grouped[:, cols, :], in_=wg_raw[:, :, cols].rearrange("p t f -> p f t")
                )
            for n in range(F_BANKS):
                cols = slice(n * BANK, (n + 1) * BANK)
                nc.vector.quantize_mx(
                    out=wg_codes[:, cols].bitcast(FP8X4),
                    scales=wg_scales[:, cols],
                    in_=wg_grouped[:, cols, :].rearrange("p f t -> p (f t)"),
                )

        def quantise_wo():
            for c in range(F_PASSES):
                nc.vector.tensor_copy(
                    out=wo_grouped[:, c, :, :].rearrange("p e (s a) -> p e s a", s=HALVES),
                    in_=wo_raw[:, c, :, :].rearrange("p (a s) e -> p e s a", s=HALVES),
                )
            for c in range(F_PASSES):
                nc.vector.quantize_mx(
                    out=wo_codes[:, c, :].bitcast(FP8X4),
                    scales=wo_scales[:, c, :],
                    in_=wo_grouped[:, c, :, :].rearrange("p e t -> p (e t)"),
                )

        sums, rms, inv_rms = {}, {}, {}
        x_t, x_grouped, x_codes, x_scales = {}, {}, {}, {}
        g_ps, h_f32, h_t, h_grouped, h_codes, h_scales = {}, {}, {}, {}, {}, {}
        out_ps = {}

        def sum_squares(j):
            grp, i = divmod(j, GROUP)
            if i == 0:
                sums[grp] = stream.tile([P, GROUP * HEADS], F32, name="sums")
            for head in range(HEADS):
                squares = stream.tile([P, DV], BF16, name="squares")
                nc.scalar.activation(
                    out=squares[:],
                    in_=o_sb[grp][:, i * F + head * DV : i * F + (head + 1) * DV],
                    func=func.Square,
                    accum_out=sums[grp][:, i * HEADS + head : i * HEADS + head + 1],
                )
            if i == GROUP - 1:
                rms[grp] = stream.tile([P, GROUP * HEADS], F32, name="rms")
                nc.scalar.activation(
                    out=rms[grp][:], in_=sums[grp][:], func=func.Sqrt, scale=1.0 / DV, bias=eps[:]
                )

        def invert_rms(j):
            grp, i = divmod(j, GROUP)
            if i == GROUP - 1:
                inv_rms[grp] = stream.tile([P, GROUP * HEADS], F32, name="inv_rms")
                nc.vector.reciprocal(out=inv_rms[grp][:], in_=rms[grp][:])

        def transpose_x(j):
            grp, i = divmod(j, GROUP)
            words = x_sb[grp][:].bitcast(F32)
            x_t[j] = psum.tile([P, 2, P], F32, name="x_t")
            for u in range(2):
                first = i * (E // 2) + u * P
                nc.tensor.transpose(x_t[j][:, u, :], words[:, first : first + P], identity[:])

        def copy_x(j):
            x_grouped[j] = stream.tile([P, P * PACK], BF16, name="x_grouped", align_bytes=64)
            nc.scalar.copy(
                out=x_grouped[j][:].bitcast(F32).rearrange("p (r u) -> p r u", u=2),
                in_=x_t[j][:].rearrange("p u r -> p r u"),
            )

        def quantise_x(j):
            x_codes[j] = stream.tile([P, P], U32, name="x_codes", align_bytes=64)
            x_scales[j] = stream.tile([P, P], U8, name="x_scales", align_bytes=64)
            nc.vector.quantize_mx(
                out=x_codes[j][:].bitcast(FP8X4), scales=x_scales[j][:], in_=x_grouped[j][:]
            )

        def gate_matmul(j):
            g_ps[j] = []
            for n in range(F_BANKS):
                cols = slice(n * BANK, (n + 1) * BANK)
                bank = psum.tile([P, BANK], F32, name="g_ps")
                nc.tensor.matmul_mx(
                    out=bank[:],
                    lhsT=x_codes[j][:].bitcast(FP8X4),
                    lhsT_scale=x_scales[j][:],
                    rhs=wg_codes[:, cols].bitcast(FP8X4),
                    rhs_scale=wg_scales[:, cols],
                    start=True,
                    stop=True,
                )
                g_ps[j].append(bank)

        def gate_multiply(j):
            grp, i = divmod(j, GROUP)
            h_f32[j] = stream.tile([P, F], F32, name="h_f32")
            for head in range(HEADS):
                n, a = divmod(head, HEADS_PER_BANK)
                nc.vector.scalar_tensor_tensor(
                    out=h_f32[j][:, head * DV : (head + 1) * DV],
                    in0=g_ps[j][n][:, a * DV : (a + 1) * DV],
                    scalar=inv_rms[grp][:, i * HEADS + head : i * HEADS + head + 1],
                    in1=o_sb[grp][:, i * F + head * DV : i * F + (head + 1) * DV],
                    op0=mult,
                    op1=mult,
                )

        def transpose_h(j):
            h_t[j] = []
            for c in range(F_PASSES):
                bank = psum.tile([P, PACK, P], F32, name="h_t")
                for s in range(HALVES):
                    for a in range(HEADS_PER_PASS):
                        first = c * K_PASS + a * DV + s * P
                        nc.tensor.transpose(
                            bank[:, s * HEADS_PER_PASS + a, :],
                            h_f32[j][:, first : first + P],
                            identity[:],
                        )
                h_t[j].append(bank)

        def scale_h(j):
            h_grouped[j] = stream.tile([P, F_PASSES, P, PACK], BF16, name="h_grouped", align_bytes=64)
            for c in range(F_PASSES):
                if (j * F_PASSES + c) % SCALAR_EVERY == SCALAR_EVERY - 1:
                    for s in range(HALVES):
                        values = slice(s * HEADS_PER_PASS, (s + 1) * HEADS_PER_PASS)
                        nc.scalar.activation(
                            out=h_grouped[j][:, c, :, values],
                            in_=h_t[j][c][:, values, :].rearrange("p a r -> p r a"),
                            func=func.Copy,
                            scale=gn_word[:, s * HEADS_PER_PASS : s * HEADS_PER_PASS + 1],
                        )
                else:
                    nc.vector.tensor_tensor(
                        out=h_grouped[j][:, c, :, :],
                        in0=h_t[j][c][:].rearrange("p t r -> p r t"),
                        in1=gn_word[:].unsqueeze(1).to_broadcast([P, P, PACK]),
                        op=mult,
                    )

        def quantise_h(j):
            h_codes[j] = stream.tile([P, F_PASSES * P], U32, name="h_codes", align_bytes=64)
            h_scales[j] = stream.tile([P, F_PASSES * P], U8, name="h_scales", align_bytes=64)
            nc.vector.quantize_mx(
                out=h_codes[j][:].bitcast(FP8X4),
                scales=h_scales[j][:],
                in_=h_grouped[j][:].rearrange("p c r t -> p (c r t)"),
            )

        def out_matmul(j):
            out_ps[j] = psum.tile([P, E], F32, name="out_ps")
            for c in range(F_PASSES):
                tokens = slice(c * P, (c + 1) * P)
                nc.tensor.matmul_mx(
                    out=out_ps[j][:],
                    lhsT=h_codes[j][:, tokens].bitcast(FP8X4),
                    lhsT_scale=h_scales[j][:, tokens],
                    rhs=wo_codes[:, c, :].bitcast(FP8X4),
                    rhs_scale=wo_scales[:, c, :],
                    start=(c == 0),
                    stop=(c == F_PASSES - 1),
                )

        def copy_out(j):
            grp, i = divmod(j, GROUP)
            out_sb = stream.tile([P, E], F32, name="out_sb")
            nc.scalar.copy(out=out_sb[:], in_=out_ps[j][:])
            nc.sync.dma_start(out=out_dram[grp][:, i * E : (i + 1) * E], in_=out_sb[:])

        def run(stage, j):
            if 0 <= j < TILES:
                stage(j)

        def pipeline_step(step):
            run(transpose_x, step + X_TRANSPOSE_LEAD)
            run(transpose_h, step + H_TRANSPOSE_LEAD)
            run(copy_x, step + X_COPY_LEAD)
            run(copy_out, step + OUT_COPY_LEAD)
            run(sum_squares, step + SQUARES_LEAD)
            run(gate_multiply, step + GATE_MULTIPLY_LEAD)
            run(gate_matmul, step + GATE_MATMUL_LEAD)
            run(invert_rms, step + INVERT_RMS_LEAD)
            run(quantise_x, step + X_QUANTISE_LEAD)
            run(quantise_h, step + H_QUANTISE_LEAD)
            run(out_matmul, step + OUT_MATMUL_LEAD)
            run(scale_h, step + H_SCALE_LEAD)

        with tc.manual_schedule():
            quantise_wg()
            for step in range(FIRST_STEP, 1):
                pipeline_step(step)
            quantise_wo()
            for step in range(1, LAST_STEP + 1):
                pipeline_step(step)
